import numpy as np
import ml_dtypes


def mxq(x, axis, fmt="e4m3"):
    dtype, down = {"e4m3": (ml_dtypes.float8_e4m3fn, 7), "e5m2": (ml_dtypes.float8_e5m2, 14)}[fmt]
    v = np.moveaxis(np.asarray(x, np.float32).astype(ml_dtypes.bfloat16).astype(np.float64), axis, -1)
    blocks = v.reshape(v.shape[:-1] + (-1, 32))
    amax = np.abs(blocks).max(-1, keepdims=True)
    byte = np.maximum(np.where(amax > 0, np.frexp(amax)[1] - 1 + 127, 0) - down, 1)
    scale = np.exp2(byte - 127.0)
    codes = (blocks / scale).astype(np.float32).astype(dtype).astype(np.float64)
    return np.moveaxis((codes * scale).reshape(v.shape), -1, axis)


WIDE = False


def mx_kscale(k):
    if not WIDE:
        return np.ones(k)
    levels = np.array([10, -10, 5, -5, 0])
    if k % 512:
        return np.exp2(np.random.permutation(np.resize(levels, k // 32))).repeat(32)
    a = np.empty((k // 512, 16))
    for p in range(k // 512):
        a[p, :8] = np.random.permutation(np.resize(levels, 8))
        for g in range(8):
            far = levels[np.abs(levels - a[p, g]) >= 10]
            a[p, g + 8] = far[np.random.randint(len(far))]
    return np.exp2(a.ravel()).repeat(32)


BF16 = ml_dtypes.bfloat16


def bf(x):
    return np.asarray(x, np.float32).astype(BF16)


def f64(x):
    return np.asarray(x).astype(np.float64)


E2M1 = np.array([0.0, 0.5, 1.0, 1.5, 2.0, 3.0, 4.0, 6.0, -0.0, -0.5, -1.0, -1.5, -2.0, -3.0, -4.0, -6.0])


def pack_weight(w, fmt):
    k, n = w.shape
    w = f64(bf(w)).reshape(k // 32, 32, n)
    amax = np.abs(w).max(1)
    if fmt == "e4m3":
        byte = np.frexp(amax)[1] - 1 + 127 - 7
    else:
        mant, ex = np.frexp(amax / 6.0)
        byte = np.where(mant > 0.5, ex, ex - 1) + 127
    byte = np.clip(np.where(amax > 0, byte, 1), 1, 254)
    scaled = (w * np.exp2(127.0 - byte)[:, None, :]).reshape(k, n).astype(np.float32)
    by_word = np.ascontiguousarray(scaled.reshape(k // 512, 128, 4, n).transpose(0, 1, 3, 2))
    if fmt == "e4m3":
        words = by_word.astype(ml_dtypes.float8_e4m3fn).view(np.uint8)
    else:
        c = by_word.astype(ml_dtypes.float4_e2m1fn).view(np.uint8) & 0xF
        words = c[..., 0::2] | (c[..., 1::2] << 4)
    return np.ascontiguousarray(words), np.ascontiguousarray(byte.astype(np.uint8).reshape(k // 512, 16, n))


def unpack_weight(words, scales, fmt):
    g, p, n, _ = words.shape
    if fmt == "e4m3":
        vals = np.ascontiguousarray(words).view(ml_dtypes.float8_e4m3fn).astype(np.float64)
    else:
        nib = np.empty((g, p, n, 4), np.uint8)
        nib[..., 0::2] = words & 0xF
        nib[..., 1::2] = words >> 4
        vals = E2M1[nib]
    vals = vals * np.repeat(np.exp2(scales.astype(np.float64) - 127.0), 8, axis=1)[..., None]
    return vals.transpose(0, 1, 3, 2).reshape(g * 512, n)
def pack4(w):
    words, scales = pack_weight(w, "e2m1")
    return words.reshape(words.shape[0], 128, -1), scales


def unpack4(words, scales):
    return unpack_weight(words.reshape(words.shape[0], 128, -1, 2), scales, "e2m1")


B, S, D, NH = 2, 512, 1024, 8
SCALE = np.sqrt(D // NH)


def draw0():
    s, t = mx_kscale(D), mx_kscale(D)
    x = bf(np.random.standard_normal((B, S, D)) * s)
    wq = np.random.standard_normal((D, D)) * 0.84 / np.sqrt(D) / s[None, :] * t[:, None]
    wk = np.random.standard_normal((D, D)) * 0.84 / np.sqrt(D) / s[None, :] / t[:, None]
    wq_words, wq_scales = pack4(wq.T)
    wk_words, wk_scales = pack4(wk.T)
    return {"x": x,
            "wq_words": wq_words, "wq_scales": wq_scales,
            "wk_words": wk_words, "wk_scales": wk_scales}


def core(x, wq_words, wq_scales, wk_words, wk_scales):
    xq = mxq(f64(x), 2, "e4m3")
    q = xq @ unpack4(wq_words, wq_scales)
    k = xq @ unpack4(wk_words, wk_scales)
    sc = (mxq(q, 2, "e4m3") @ mxq(k, 2, "e4m3").transpose(0, 2, 1)) / SCALE
    e = np.exp(sc - sc.max(-1, keepdims=True))
    return e / e.sum(-1, keepdims=True)


def e4m3fn_bytes(y):
    return np.clip(np.asarray(y, np.float64), -448.0, 448.0).astype(np.float32).astype(ml_dtypes.float8_e4m3fn).view(np.uint8)


def e4m3fn_values(b):
    return np.asarray(b, np.uint8).view(ml_dtypes.float8_e4m3fn).astype(np.float64)


def setup_inputs():
    d = draw0()
    x0 = np.asarray(d['x']).astype(np.float64)
    s = (np.max(np.abs(x0), axis=(0, 1), keepdims=True) / 448.0).astype(np.float32)
    out = {}
    for k, v in d.items():
        if k == 'x':
            out['x_bytes'] = e4m3fn_bytes(x0 / s.astype(np.float64))
            out['x_scale'] = s
        else:
            out[k] = v
    return out


def reference(x_bytes, x_scale, wq_words, wq_scales, wk_words, wk_scales):
    return core(e4m3fn_values(x_bytes) * x_scale.astype(np.float64), wq_words, wq_scales, wk_words, wk_scales)

@@ -1,0 +1,274 @@
+import math
+from contextlib import ExitStack
+
+import concourse.mybir as mybir
+from concourse.masks import make_identity
+
+F32 = mybir.dt.float32
+BF16 = mybir.dt.bfloat16
+I32 = mybir.dt.int32
+U32 = mybir.dt.uint32
+U8 = mybir.dt.uint8
+FP8 = mybir.dt.float8_e4m3fn
+FP8X4 = mybir.dt.float8_e4m3fn_x4
+FP4X4 = mybir.dt.float4_e2m1fn_x4
+ACT = mybir.ActivationFunctionType
+ALU = mybir.AluOpType
+AX = mybir.AxisListType
+
+B, S, D = 2, 512, 1024
+P = 128
+TILES = B * S // P
+PER_BATCH = S // P
+PASSES = D // 512
+INV = 1.0 / math.sqrt(128.0)
+FLOPS = 2 * 2 * B * S * D * D + 2 * B * S * S * D
+
+SEQ = ["T0","T1","T2","K0","K1","T3","T4","Q0","Q1","K2","Q2","K3","T5","T6","K4","Q4","Q3","S0","T7","K6","K5","S1","Q5","S2","K7","S3","Q6","S4","Q7","S5","S6","S7"]
+CAST_V = (0,)
+EXIT_V = (("K3",1,),)
+NEG_S = (7,6,)
+NORM_G = (4,)
+LAG_CAST = 4
+LAG_SCALE = 1
+LAG_QUANT = 0
+LAG_MAX = 0
+LAG_EXP = 1
+LAG_NORM = 2
+XFIRST = 3
+
+
+def tile_attentionnet_pa_w4_kernel(tc, x_bytes, x_scale, wq_words, wq_scales, wk_words, wk_scales, out):
+    nc = tc.nc
+    x_rows = x_bytes.rearrange("b s d -> (b s) d")
+    out_rows = out.rearrange("b s t -> (b s) t")
+
+    with ExitStack() as ctx:
+        keep = ctx.enter_context(tc.tile_pool(name="keep", bufs=1))
+        work = ctx.enter_context(tc.tile_pool(name="work", bufs=3))
+        soft = ctx.enter_context(tc.tile_pool(name="soft", bufs=4))
+        banks = ctx.enter_context(tc.psum_pool(name="banks", bufs=8))
+
+        warm = keep.tile([P, 1], F32, name="warm")
+        warm_out = keep.tile([P, 1], F32, name="warm_out")
+        ident = keep.tile([P, P], F32, name="ident")
+        scale_t = keep.tile([P, PASSES * 4], F32, name="scale_t")
+        xb = [keep.tile([P, D], U8, name="xb%d" % i) for i in range(TILES)]
+        raw = {m: keep.tile([P, 4096], U8, name="raw_" + m, align_bytes=64) for m in "KQ"}
+        raw_s = {m: keep.tile([P, 2048], U8, name="raws_" + m, align_bytes=64) for m in "KQ"}
+        wts = {m: keep.tile([P, 4096], U8, name="wts_" + m, align_bytes=64) for m in "KQ"}
+        wts_s = {m: keep.tile([P, 2048], U8, name="wtss_" + m, align_bytes=64) for m in "KQ"}
+        xc = [keep.tile([P, 256], U32, name="xc%d" % i, align_bytes=64) for i in range(TILES)]
+        xs = [keep.tile([P, 256], U8, name="xs%d" % i, align_bytes=64) for i in range(TILES)]
+        kc = [keep.tile([P, 1024], U32, name="kc%d" % i, align_bytes=64) for i in range(B)]
+        ks = [keep.tile([P, 1024], U8, name="ks%d" % i, align_bytes=64) for i in range(B)]
+        qc = [keep.tile([P, 256], U32, name="qc%d" % i, align_bytes=64) for i in range(TILES)]
+        qs = [keep.tile([P, 256], U8, name="qs%d" % i, align_bytes=64) for i in range(TILES)]
+
+        hbm_w = {"K": wk_words, "Q": wq_words}
+        hbm_s = {"K": wk_scales, "Q": wq_scales}
+
+        def load_x(i):
+            nc.sync.dma_start(out=xb[i][:], in_=x_rows[i * P : (i + 1) * P, :])
+
+        def load_w(m):
+            nc.sync.dma_start(
+                out=raw[m][:].bitcast(I32).rearrange("p (g n) -> p g n", g=PASSES),
+                in_=hbm_w[m].bitcast(I32).rearrange("g p n -> p g n"),
+            )
+
+        def load_s(m):
+            dst = raw_s[m][:].bitcast(I32).rearrange("p (g n) -> p g n", g=PASSES)
+            src = hbm_s[m].bitcast(I32)
+            for q in range(4):
+                nc.sync.dma_start(out=dst[32 * q : 32 * q + 4], in_=src[:, 4 * q : 4 * q + 4, :].rearrange("g r n -> r g n"))
+
+        def permute(m):
+            nc.vector.tensor_copy(
+                out=wts[m][:].bitcast(I32).rearrange("p (t c w) -> p t c w", t=4, w=4),
+                in_=raw[m][:].bitcast(I32).rearrange("p (c t w) -> p t c w", t=4, w=4),
+            )
+
+        def permute_s(m):
+            nc.vector.tensor_copy(
+                out=wts_s[m][:].bitcast(I32).rearrange("p (t c w) -> p t c w", t=4, w=2),
+                in_=raw_s[m][:].bitcast(I32).rearrange("p (c t w) -> p t c w", t=4, w=2),
+            )
+
+        xbf = {}
+        xt = {}
+        xg = {}
+        yp = {}
+        yg = {}
+        sp = {}
+        ex = {}
+
+        def cast(i):
+            xbf[i] = work.tile([P, D], BF16, name="xbf", align_bytes=64)
+            src = xb[i][:].bitcast(FP8)
+            if i in CAST_V:
+                nc.vector.tensor_copy(out=xbf[i][:], in_=src)
+            else:
+                nc.scalar.copy(xbf[i][:], src)
+
+        def turn(i):
+            xt[i] = banks.tile([P, 512], F32, name="bank")
+            words = xbf[i][:].bitcast(F32)
+            for g in range(PASSES):
+                for u in range(2):
+                    nc.tensor.transpose(
+                        xt[i][:, g * 256 + u * 128 : g * 256 + u * 128 + 128],
+                        words[:, 256 * g + u : 256 * (g + 1) : 2],
+                        ident[:],
+                    )
+
+        def scale(i, g):
+            if g == 0:
+                xg[i] = work.tile([P, 1024], BF16, name="xg", align_bytes=64)
+            nc.vector.tensor_tensor(
+                out=xg[i][:, g * 512 : (g + 1) * 512].rearrange("p (r u e) -> p r u e", u=2, e=2),
+                in0=xt[i][:, g * 256 : (g + 1) * 256].bitcast(BF16).rearrange("p (u r e) -> p r u e", u=2, e=2),
+                in1=scale_t[:, g * 4 : (g + 1) * 4].rearrange("p (u e) -> p u e", e=2).unsqueeze(1).to_broadcast([P, P, 2, 2]),
+                op=ALU.mult,
+            )
+
+        def quant_x(i):
+            nc.vector.quantize_mx(out=xc[i][:].bitcast(FP8X4), scales=xs[i][:], in_=xg[i][:])
+
+        def project(m, i, h):
+            yp[m, i, h] = banks.tile([P, 512], F32, name="bank")
+            for t in range(4):
+                for g in range(PASSES):
+                    c = 2 * g + h
+                    nc.tensor.matmul_mx(
+                        out=yp[m, i, h][:, t * P : (t + 1) * P],
+                        lhsT=wts[m][:, t * 1024 + c * 256 : t * 1024 + (c + 1) * 256].bitcast(FP4X4),
+                        lhsT_scale=wts_s[m][:, t * 512 + c * 128 : t * 512 + (c + 1) * 128],
+                        rhs=xc[i][:, g * P : (g + 1) * P].bitcast(FP8X4),
+                        rhs_scale=xs[i][:, g * P : (g + 1) * P],
+                        start=(g == 0),
+                        stop=(g == PASSES - 1),
+                    )
+
+        def leave(m, i, h):
+            if h == 0:
+                yg[m, i] = work.tile([P, 1024], BF16, name="yg", align_bytes=64)
+            dst = yg[m, i][:, h * 512 : (h + 1) * 512].rearrange("p (n t) -> p n t", t=4)
+            bank = yp[m, i, h][:].rearrange("p (t n) -> p n t", t=4)
+            if (m + str(i), h) in EXIT_V:
+                nc.vector.tensor_copy(out=dst, in_=bank)
+            else:
+                nc.scalar.copy(dst, bank)
+
+        def quant_y(m, i):
+            b, j = divmod(i, PER_BATCH)
+            if m == "Q":
+                nc.vector.quantize_mx(out=qc[i][:].bitcast(FP8X4), scales=qs[i][:], in_=yg[m, i][:])
+            else:
+                for h in range(2):
+                    cols = slice(h * S + j * P, h * S + (j + 1) * P)
+                    nc.vector.quantize_mx(out=kc[b][:, cols].bitcast(FP8X4), scales=ks[b][:, cols], in_=yg[m, i][:, h * 512 : (h + 1) * 512])
+
+        def score(i):
+            b = i // PER_BATCH
+            sp[i] = banks.tile([P, S], F32, name="bank")
+            for h in range(2):
+                nc.tensor.matmul_mx(
+                    out=sp[i][:],
+                    lhsT=qc[i][:, h * P : (h + 1) * P].bitcast(FP8X4),
+                    lhsT_scale=qs[i][:, h * P : (h + 1) * P],
+                    rhs=kc[b][:, h * S : (h + 1) * S].bitcast(FP8X4),
+                    rhs_scale=ks[b][:, h * S : (h + 1) * S],
+                    start=(h == 0),
+                    stop=(h == 1),
+                )
+
+        def row_max(i):
+            mx = soft.tile([P, 1], F32, name="mx")
+            nb = soft.tile([P, 1], F32, name="nb")
+            nc.vector.tensor_reduce(out=mx[:], in_=sp[i][:], axis=AX.X, op=ALU.max)
+            if i in NEG_S:
+                nc.scalar.mul(nb[:], mx[:], -INV)
+            else:
+                nc.gpsimd.tensor_scalar(out=nb[:], in0=mx[:], scalar1=-INV, scalar2=None, op0=ALU.mult)
+            ex[i] = [nb]
+
+        def exps(i):
+            e = soft.tile([P, S], F32, name="e")
+            sm = soft.tile([P, 1], F32, name="sm")
+            nc.scalar.activation(out=e[:], in_=sp[i][:], func=ACT.Exp, bias=ex[i][0][:], scale=INV, accum_out=sm[:])
+            ex[i] = [e, sm]
+
+        def finish(i):
+            e, sm = ex[i]
+            rc = soft.tile([P, 1], F32, name="rc")
+            o = soft.tile([P, S], F32, name="o")
+            nc.vector.reciprocal(rc[:], sm[:])
+            if i in NORM_G:
+                nc.gpsimd.tensor_scalar(out=o[:], in0=e[:], scalar1=rc[:], scalar2=0.0, op0=ALU.mult, op1=ALU.add)
+            else:
+                nc.vector.tensor_scalar(out=o[:], in0=e[:], scalar1=rc[:], scalar2=None, op0=ALU.mult)
+            nc.sync.dma_start(out=out_rows[i * P : (i + 1) * P, :], in_=o[:])
+
+        ctx.enter_context(tc.manual_schedule())
+        nc.vector.memset(warm[:], 0.0)
+        nc.scalar.activation(out=warm_out[:], in_=warm[:], func=ACT.Exp)
+        nc.vector.memset(raw_s["K"][:].bitcast(I32), 0)
+        nc.vector.memset(raw_s["Q"][:].bitcast(I32), 0)
+        load_x(0)
+        nc.scalar.dma_start(out=scale_t[:].rearrange("p (g t) -> p g t", t=4), in_=x_scale.rearrange("a b (g p t) -> p (a b g) t", p=P, t=4))
+        for i in range(1, XFIRST):
+            load_x(i)
+        load_w("K")
+        load_s("K")
+        load_x(XFIRST)
+        load_w("Q")
+        load_s("Q")
+        for i in range(XFIRST + 1, TILES):
+            load_x(i)
+        make_identity(nc, ident[:])
+
+        pending = {}
+
+        def later(n, fn, *args):
+            pending.setdefault(n, []).append((fn, args))
+
+        for n, op in enumerate(SEQ):
+            kind, i = op[0], int(op[1])
+            if kind == "T":
+                later(max(n - LAG_CAST, -1), cast, i)
+                later(n + LAG_SCALE, scale, i, 0)
+                later(n + LAG_SCALE, scale, i, 1)
+                if i == 0:
+                    later(n + LAG_SCALE, permute, "K")
+                later(n + LAG_SCALE, quant_x, i)
+                if i == 0:
+                    later(n + LAG_SCALE, permute_s, "K")
+                if i == 1:
+                    later(n + LAG_SCALE, permute, "Q")
+                    later(n + LAG_SCALE, permute_s, "Q")
+            elif kind == "S":
+                later(n + LAG_MAX, row_max, i)
+                later(n + LAG_MAX + LAG_EXP, exps, i)
+                later(n + LAG_MAX + LAG_EXP + LAG_NORM, finish, i)
+            else:
+                later(n + LAG_QUANT, quant_y, kind, i)
+
+        def run_pending(n):
+            for fn, args in pending.get(n, []):
+                fn(*args)
+
+        run_pending(-1)
+        for n, op in enumerate(SEQ):
+            kind, i = op[0], int(op[1])
+            if kind == "T":
+                turn(i)
+            elif kind == "S":
+                score(i)
+            else:
+                for h in range(2):
+                    project(kind, i, h)
+                    leave(kind, i, h)
+            run_pending(n)
+        for n in range(len(SEQ), len(SEQ) + 6):
+            run_pending(n)

@@ -24,18 +24,22 @@ PASSES = D // 512
 INV = 1.0 / math.sqrt(128.0)
 FLOPS = 2 * 2 * B * S * D * D + 2 * B * S * S * D
 
-SEQ = ["T0","T1","T2","K0","K1","T3","T4","Q0","Q1","K2","Q2","K3","T5","T6","K4","Q4","Q3","S0","T7","K6","K5","S1","Q5","S2","K7","S3","Q6","S4","Q7","S5","S6","S7"]
-CAST_V = (0,)
-EXIT_V = (("K3",1,),)
-NEG_S = (7,6,)
-NORM_G = (4,)
+SEQ = ["D","D","D","T0","T1","D","D","T2","K0","T3","K1","K2","Q1","T4","T5","Q0","T6","T7","K3","Q2","Q4","Q3","S0","K4","K6","S1","K5","S3","K7","S2","Q5","S4","Q6","S5","Q7","S6","S7"]
+CAST_V = (0,1,4,6,)
+EXIT_V = ()
+NORM_G = ()
 LAG_CAST = 4
 LAG_SCALE = 1
 LAG_QUANT = 0
 LAG_MAX = 0
-LAG_EXP = 1
-LAG_NORM = 2
+LAG_EXP = 2
+LAG_INV = 1
+LAG_NORM = 1
 XFIRST = 3
+PERM_Q = 8
+CAST_SPLIT = (0,)
+NORM_SPLIT = (7,)
+NORM_COLS = 320
 
 
 def tile_attentionnet_pa_w4_kernel(tc, x_bytes, x_scale, wq_words, wq_scales, wk_words, wk_scales, out):
@@ -45,12 +49,14 @@ def tile_attentionnet_pa_w4_kernel(tc, x_bytes, x_scale, wq_words, wq_scales, wk
 
     with ExitStack() as ctx:
         keep = ctx.enter_context(tc.tile_pool(name="keep", bufs=1))
-        work = ctx.enter_context(tc.tile_pool(name="work", bufs=3))
+        work = ctx.enter_context(tc.tile_pool(name="work", bufs=5))
         soft = ctx.enter_context(tc.tile_pool(name="soft", bufs=4))
         banks = ctx.enter_context(tc.psum_pool(name="banks", bufs=8))
 
         warm = keep.tile([P, 1], F32, name="warm")
         warm_out = keep.tile([P, 1], F32, name="warm_out")
+        zeros = keep.tile([P, 512], BF16, name="zeros")
+        dummy = banks.tile([P, 512], F32, name="bank")
         ident = keep.tile([P, P], F32, name="ident")
         scale_t = keep.tile([P, PASSES * 4], F32, name="scale_t")
         xb = [keep.tile([P, D], U8, name="xb%d" % i) for i in range(TILES)]
@@ -71,10 +77,10 @@ def tile_attentionnet_pa_w4_kernel(tc, x_bytes, x_scale, wq_words, wq_scales, wk
         def load_x(i):
             nc.sync.dma_start(out=xb[i][:], in_=x_rows[i * P : (i + 1) * P, :])
 
-        def load_w(m):
+        def load_w(m, h):
             nc.sync.dma_start(
-                out=raw[m][:].bitcast(I32).rearrange("p (g n) -> p g n", g=PASSES),
-                in_=hbm_w[m].bitcast(I32).rearrange("g p n -> p g n"),
+                out=raw[m][:].bitcast(I32)[:, h * 512 : (h + 1) * 512].rearrange("p (g n) -> p g n", g=PASSES),
+                in_=hbm_w[m].bitcast(I32)[:, :, h * 256 : (h + 1) * 256].rearrange("g p n -> p g n"),
             )
 
         def load_s(m):
@@ -83,17 +89,21 @@ def tile_attentionnet_pa_w4_kernel(tc, x_bytes, x_scale, wq_words, wq_scales, wk
             for q in range(4):
                 nc.sync.dma_start(out=dst[32 * q : 32 * q + 4], in_=src[:, 4 * q : 4 * q + 4, :].rearrange("g r n -> r g n"))
 
-        def permute(m):
+        def permute(m, h):
+            half = slice(h * 512, (h + 1) * 512)
             nc.vector.tensor_copy(
-                out=wts[m][:].bitcast(I32).rearrange("p (t c w) -> p t c w", t=4, w=4),
-                in_=raw[m][:].bitcast(I32).rearrange("p (c t w) -> p t c w", t=4, w=4),
+                out=wts[m][:].bitcast(I32)[:, half].rearrange("p (t c w) -> p t c w", t=4, w=4),
+                in_=raw[m][:].bitcast(I32)[:, half].rearrange("p (c t w) -> p t c w", t=4, w=4),
             )
 
-        def permute_s(m):
-            nc.vector.tensor_copy(
-                out=wts_s[m][:].bitcast(I32).rearrange("p (t c w) -> p t c w", t=4, w=2),
-                in_=raw_s[m][:].bitcast(I32).rearrange("p (c t w) -> p t c w", t=4, w=2),
-            )
+        def permute_s(m, h):
+            src = raw_s[m][:].bitcast(I32)
+            dst = wts_s[m][:].bitcast(I32)
+            for g in range(PASSES):
+                nc.gpsimd.tensor_copy(
+                    out=dst[:, h * 256 + g * 128 : h * 256 + (g + 1) * 128].rearrange("p (t c w) -> p t c w", t=4, w=2),
+                    in_=src[:, g * 256 + h * 128 : g * 256 + (h + 1) * 128].rearrange("p (c t w) -> p t c w", t=4, w=2),
+                )
 
         xbf = {}
         xt = {}
@@ -106,7 +116,10 @@ def tile_attentionnet_pa_w4_kernel(tc, x_bytes, x_scale, wq_words, wq_scales, wk
         def cast(i):
             xbf[i] = work.tile([P, D], BF16, name="xbf", align_bytes=64)
             src = xb[i][:].bitcast(FP8)
-            if i in CAST_V:
+            if i in CAST_SPLIT:
+                nc.vector.tensor_copy(out=xbf[i][:, 0:512], in_=xb[i][:, 0:512].bitcast(FP8))
+                nc.scalar.copy(xbf[i][:, 512:1024], xb[i][:, 512:1024].bitcast(FP8))
+            elif i in CAST_V:
                 nc.vector.tensor_copy(out=xbf[i][:], in_=src)
             else:
                 nc.scalar.copy(xbf[i][:], src)
@@ -133,17 +146,19 @@ def tile_attentionnet_pa_w4_kernel(tc, x_bytes, x_scale, wq_words, wq_scales, wk
             )
 
         def quant_x(i):
-            nc.vector.quantize_mx(out=xc[i][:].bitcast(FP8X4), scales=xs[i][:], in_=xg[i][:])
+            for g in range(PASSES):
+                cols = slice(g * P, (g + 1) * P)
+                nc.vector.quantize_mx(out=xc[i][:, cols].bitcast(FP8X4), scales=xs[i][:, cols], in_=xg[i][:, g * 512 : (g + 1) * 512])
 
         def project(m, i, h):
             yp[m, i, h] = banks.tile([P, 512], F32, name="bank")
             for t in range(4):
                 for g in range(PASSES):
-                    c = 2 * g + h
+                    plane = h * 1024 + g * 512
                     nc.tensor.matmul_mx(
                         out=yp[m, i, h][:, t * P : (t + 1) * P],
-                        lhsT=wts[m][:, t * 1024 + c * 256 : t * 1024 + (c + 1) * 256].bitcast(FP4X4),
-                        lhsT_scale=wts_s[m][:, t * 512 + c * 128 : t * 512 + (c + 1) * 128],
+                        lhsT=wts[m][:, h * 2048 + t * 512 + g * 256 : h * 2048 + t * 512 + (g + 1) * 256].bitcast(FP4X4),
+                        lhsT_scale=wts_s[m][:, plane + t * 128 : plane + (t + 1) * 128],
                         rhs=xc[i][:, g * P : (g + 1) * P].bitcast(FP8X4),
                         rhs_scale=xs[i][:, g * P : (g + 1) * P],
                         start=(g == 0),
@@ -187,23 +202,32 @@ def tile_attentionnet_pa_w4_kernel(tc, x_bytes, x_scale, wq_words, wq_scales, wk
             mx = soft.tile([P, 1], F32, name="mx")
             nb = soft.tile([P, 1], F32, name="nb")
             nc.vector.tensor_reduce(out=mx[:], in_=sp[i][:], axis=AX.X, op=ALU.max)
-            if i in NEG_S:
-                nc.scalar.mul(nb[:], mx[:], -INV)
-            else:
-                nc.gpsimd.tensor_scalar(out=nb[:], in0=mx[:], scalar1=-INV, scalar2=None, op0=ALU.mult)
-            ex[i] = [nb]
+            ex[i] = [mx, nb]
 
         def exps(i):
+            mx, nb = ex[i]
+            nc.scalar.mul(nb[:], mx[:], -INV)
             e = soft.tile([P, S], F32, name="e")
             sm = soft.tile([P, 1], F32, name="sm")
-            nc.scalar.activation(out=e[:], in_=sp[i][:], func=ACT.Exp, bias=ex[i][0][:], scale=INV, accum_out=sm[:])
+            nc.scalar.activation(out=e[:], in_=sp[i][:], func=ACT.Exp, bias=nb[:], scale=INV, accum_out=sm[:])
             ex[i] = [e, sm]
 
-        def finish(i):
+        def invert(i):
             e, sm = ex[i]
             rc = soft.tile([P, 1], F32, name="rc")
-            o = soft.tile([P, S], F32, name="o")
             nc.vector.reciprocal(rc[:], sm[:])
+            ex[i] = (e, rc)
+
+        def finish(i):
+            e, rc = ex[i]
+            o = soft.tile([P, S], F32, name="o")
+            if i in NORM_SPLIT:
+                lo, hi = slice(0, NORM_COLS), slice(NORM_COLS, S)
+                nc.scalar.activation(out=o[:, hi], in_=e[:, hi], func=ACT.Copy, scale=rc[:])
+                nc.vector.tensor_scalar(out=o[:, lo], in0=e[:, lo], scalar1=rc[:], scalar2=None, op0=ALU.mult)
+                nc.scalar.dma_start(out=out_rows[i * P : (i + 1) * P, hi], in_=o[:, hi])
+                nc.sync.dma_start(out=out_rows[i * P : (i + 1) * P, lo], in_=o[:, lo])
+                return
             if i in NORM_G:
                 nc.gpsimd.tensor_scalar(out=o[:], in0=e[:], scalar1=rc[:], scalar2=0.0, op0=ALU.mult, op1=ALU.add)
             else:
@@ -211,22 +235,28 @@ def tile_attentionnet_pa_w4_kernel(tc, x_bytes, x_scale, wq_words, wq_scales, wk
             nc.sync.dma_start(out=out_rows[i * P : (i + 1) * P, :], in_=o[:])
 
         ctx.enter_context(tc.manual_schedule())
+        make_identity(nc, ident[:])
         nc.vector.memset(warm[:], 0.0)
         nc.scalar.activation(out=warm_out[:], in_=warm[:], func=ACT.Exp)
         nc.vector.memset(raw_s["K"][:].bitcast(I32), 0)
+        nc.vector.memset(zeros[:], 0.0)
         nc.vector.memset(raw_s["Q"][:].bitcast(I32), 0)
         load_x(0)
         nc.scalar.dma_start(out=scale_t[:].rearrange("p (g t) -> p g t", t=4), in_=x_scale.rearrange("a b (g p t) -> p (a b g) t", p=P, t=4))
         for i in range(1, XFIRST):
             load_x(i)
-        load_w("K")
         load_s("K")
+        load_w("K", 0)
+        load_w("K", 1)
         load_x(XFIRST)
-        load_w("Q")
+        load_w("Q", 0)
+        load_w("Q", 1)
         load_s("Q")
         for i in range(XFIRST + 1, TILES):
             load_x(i)
-        make_identity(nc, ident[:])
+        for m in "KQ":
+            for h in range(2):
+                permute_s(m, h)
 
         pending = {}
 
@@ -234,23 +264,23 @@ def tile_attentionnet_pa_w4_kernel(tc, x_bytes, x_scale, wq_words, wq_scales, wk
             pending.setdefault(n, []).append((fn, args))
 
         for n, op in enumerate(SEQ):
-            kind, i = op[0], int(op[1])
+            kind, i = op[0], int(op[1:] or 0)
+            if kind == "D":
+                continue
             if kind == "T":
                 later(max(n - LAG_CAST, -1), cast, i)
                 later(n + LAG_SCALE, scale, i, 0)
                 later(n + LAG_SCALE, scale, i, 1)
                 if i == 0:
-                    later(n + LAG_SCALE, permute, "K")
+                    later(n + LAG_SCALE, permute, "K", 0)
                 later(n + LAG_SCALE, quant_x, i)
                 if i == 0:
-                    later(n + LAG_SCALE, permute_s, "K")
-                if i == 1:
-                    later(n + LAG_SCALE, permute, "Q")
-                    later(n + LAG_SCALE, permute_s, "Q")
+                    later(n + LAG_SCALE, permute, "K", 1)
             elif kind == "S":
                 later(n + LAG_MAX, row_max, i)
                 later(n + LAG_MAX + LAG_EXP, exps, i)
-                later(n + LAG_MAX + LAG_EXP + LAG_NORM, finish, i)
+                later(n + LAG_MAX + LAG_EXP + LAG_INV, invert, i)
+                later(n + LAG_MAX + LAG_EXP + LAG_INV + LAG_NORM, finish, i)
             else:
                 later(n + LAG_QUANT, quant_y, kind, i)
 
@@ -258,10 +288,14 @@ def tile_attentionnet_pa_w4_kernel(tc, x_bytes, x_scale, wq_words, wq_scales, wk
             for fn, args in pending.get(n, []):
                 fn(*args)
 
+        later(PERM_Q, permute, "Q", 0)
+        later(PERM_Q, permute, "Q", 1)
         run_pending(-1)
         for n, op in enumerate(SEQ):
-            kind, i = op[0], int(op[1])
-            if kind == "T":
+            kind, i = op[0], int(op[1:] or 0)
+            if kind == "D":
+                nc.tensor.matmul(dummy[:], zeros[:, 0:P], zeros[:], start=True, stop=True)
+            elif kind == "T":
                 turn(i)
             elif kind == "S":
                 score(i)
@@ -270,5 +304,5 @@ def tile_attentionnet_pa_w4_kernel(tc, x_bytes, x_scale, wq_words, wq_scales, wk
                     project(kind, i, h)
                     leave(kind, i, h)
             run_pending(n)
-        for n in range(len(SEQ), len(SEQ) + 6):
+        for n in range(len(SEQ), len(SEQ) + 9):
             run_pending(n)

import math
from contextlib import ExitStack

import concourse.mybir as mybir
from concourse.masks import make_identity

F32 = mybir.dt.float32
BF16 = mybir.dt.bfloat16
I32 = mybir.dt.int32
U32 = mybir.dt.uint32
U8 = mybir.dt.uint8
FP8 = mybir.dt.float8_e4m3fn
FP8X4 = mybir.dt.float8_e4m3fn_x4
FP4X4 = mybir.dt.float4_e2m1fn_x4
ACT = mybir.ActivationFunctionType
ALU = mybir.AluOpType
AX = mybir.AxisListType

B, S, D = 2, 512, 1024
P = 128
TILES = B * S // P
PER_BATCH = S // P
PASSES = D // 512
INV = 1.0 / math.sqrt(128.0)
FLOPS = 2 * 2 * B * S * D * D + 2 * B * S * S * D

SEQ = ["D","D","D","T0","T1","D","D","T2","K0","T3","K1","K2","Q1","T4","T5","Q0","T6","T7","K3","Q2","Q4","Q3","S0","K4","K6","S1","K5","S3","K7","S2","Q5","S4","Q6","S5","Q7","S6","S7"]
CAST_V = (0,1,4,6,)
EXIT_V = ()
NORM_G = ()
LAG_CAST = 4
LAG_SCALE = 1
LAG_QUANT = 0
LAG_MAX = 0
LAG_EXP = 2
LAG_INV = 1
LAG_NORM = 1
XFIRST = 3
PERM_Q = 8
CAST_SPLIT = (0,)
NORM_SPLIT = (7,)
NORM_COLS = 320


def tile_attentionnet_pa_w4_kernel(tc, x_bytes, x_scale, wq_words, wq_scales, wk_words, wk_scales, out):
    nc = tc.nc
    x_rows = x_bytes.rearrange("b s d -> (b s) d")
    out_rows = out.rearrange("b s t -> (b s) t")

    with ExitStack() as ctx:
        keep = ctx.enter_context(tc.tile_pool(name="keep", bufs=1))
        work = ctx.enter_context(tc.tile_pool(name="work", bufs=5))
        soft = ctx.enter_context(tc.tile_pool(name="soft", bufs=4))
        banks = ctx.enter_context(tc.psum_pool(name="banks", bufs=8))

        warm = keep.tile([P, 1], F32, name="warm")
        warm_out = keep.tile([P, 1], F32, name="warm_out")
        zeros = keep.tile([P, 512], BF16, name="zeros")
        dummy = banks.tile([P, 512], F32, name="bank")
        ident = keep.tile([P, P], F32, name="ident")
        scale_t = keep.tile([P, PASSES * 4], F32, name="scale_t")
        xb = [keep.tile([P, D], U8, name="xb%d" % i) for i in range(TILES)]
        raw = {m: keep.tile([P, 4096], U8, name="raw_" + m, align_bytes=64) for m in "KQ"}
        raw_s = {m: keep.tile([P, 2048], U8, name="raws_" + m, align_bytes=64) for m in "KQ"}
        wts = {m: keep.tile([P, 4096], U8, name="wts_" + m, align_bytes=64) for m in "KQ"}
        wts_s = {m: keep.tile([P, 2048], U8, name="wtss_" + m, align_bytes=64) for m in "KQ"}
        xc = [keep.tile([P, 256], U32, name="xc%d" % i, align_bytes=64) for i in range(TILES)]
        xs = [keep.tile([P, 256], U8, name="xs%d" % i, align_bytes=64) for i in range(TILES)]
        kc = [keep.tile([P, 1024], U32, name="kc%d" % i, align_bytes=64) for i in range(B)]
        ks = [keep.tile([P, 1024], U8, name="ks%d" % i, align_bytes=64) for i in range(B)]
        qc = [keep.tile([P, 256], U32, name="qc%d" % i, align_bytes=64) for i in range(TILES)]
        qs = [keep.tile([P, 256], U8, name="qs%d" % i, align_bytes=64) for i in range(TILES)]

        hbm_w = {"K": wk_words, "Q": wq_words}
        hbm_s = {"K": wk_scales, "Q": wq_scales}

        def load_x(i):
            nc.sync.dma_start(out=xb[i][:], in_=x_rows[i * P : (i + 1) * P, :])

        def load_w(m, h):
            nc.sync.dma_start(
                out=raw[m][:].bitcast(I32)[:, h * 512 : (h + 1) * 512].rearrange("p (g n) -> p g n", g=PASSES),
                in_=hbm_w[m].bitcast(I32)[:, :, h * 256 : (h + 1) * 256].rearrange("g p n -> p g n"),
            )

        def load_s(m):
            dst = raw_s[m][:].bitcast(I32).rearrange("p (g n) -> p g n", g=PASSES)
            src = hbm_s[m].bitcast(I32)
            for q in range(4):
                nc.sync.dma_start(out=dst[32 * q : 32 * q + 4], in_=src[:, 4 * q : 4 * q + 4, :].rearrange("g r n -> r g n"))

        def permute(m, h):
            half = slice(h * 512, (h + 1) * 512)
            nc.vector.tensor_copy(
                out=wts[m][:].bitcast(I32)[:, half].rearrange("p (t c w) -> p t c w", t=4, w=4),
                in_=raw[m][:].bitcast(I32)[:, half].rearrange("p (c t w) -> p t c w", t=4, w=4),
            )

        def permute_s(m, h):
            src = raw_s[m][:].bitcast(I32)
            dst = wts_s[m][:].bitcast(I32)
            for g in range(PASSES):
                nc.gpsimd.tensor_copy(
                    out=dst[:, h * 256 + g * 128 : h * 256 + (g + 1) * 128].rearrange("p (t c w) -> p t c w", t=4, w=2),
                    in_=src[:, g * 256 + h * 128 : g * 256 + (h + 1) * 128].rearrange("p (c t w) -> p t c w", t=4, w=2),
                )

        xbf = {}
        xt = {}
        xg = {}
        yp = {}
        yg = {}
        sp = {}
        ex = {}

        def cast(i):
            xbf[i] = work.tile([P, D], BF16, name="xbf", align_bytes=64)
            src = xb[i][:].bitcast(FP8)
            if i in CAST_SPLIT:
                nc.vector.tensor_copy(out=xbf[i][:, 0:512], in_=xb[i][:, 0:512].bitcast(FP8))
                nc.scalar.copy(xbf[i][:, 512:1024], xb[i][:, 512:1024].bitcast(FP8))
            elif i in CAST_V:
                nc.vector.tensor_copy(out=xbf[i][:], in_=src)
            else:
                nc.scalar.copy(xbf[i][:], src)

        def turn(i):
            xt[i] = banks.tile([P, 512], F32, name="bank")
            words = xbf[i][:].bitcast(F32)
            for g in range(PASSES):
                for u in range(2):
                    nc.tensor.transpose(
                        xt[i][:, g * 256 + u * 128 : g * 256 + u * 128 + 128],
                        words[:, 256 * g + u : 256 * (g + 1) : 2],
                        ident[:],
                    )

        def scale(i, g):
            if g == 0:
                xg[i] = work.tile([P, 1024], BF16, name="xg", align_bytes=64)
            nc.vector.tensor_tensor(
                out=xg[i][:, g * 512 : (g + 1) * 512].rearrange("p (r u e) -> p r u e", u=2, e=2),
                in0=xt[i][:, g * 256 : (g + 1) * 256].bitcast(BF16).rearrange("p (u r e) -> p r u e", u=2, e=2),
                in1=scale_t[:, g * 4 : (g + 1) * 4].rearrange("p (u e) -> p u e", e=2).unsqueeze(1).to_broadcast([P, P, 2, 2]),
                op=ALU.mult,
            )

        def quant_x(i):
            for g in range(PASSES):
                cols = slice(g * P, (g + 1) * P)
                nc.vector.quantize_mx(out=xc[i][:, cols].bitcast(FP8X4), scales=xs[i][:, cols], in_=xg[i][:, g * 512 : (g + 1) * 512])

        def project(m, i, h):
            yp[m, i, h] = banks.tile([P, 512], F32, name="bank")
            for t in range(4):
                for g in range(PASSES):
                    plane = h * 1024 + g * 512
                    nc.tensor.matmul_mx(
                        out=yp[m, i, h][:, t * P : (t + 1) * P],
                        lhsT=wts[m][:, h * 2048 + t * 512 + g * 256 : h * 2048 + t * 512 + (g + 1) * 256].bitcast(FP4X4),
                        lhsT_scale=wts_s[m][:, plane + t * 128 : plane + (t + 1) * 128],
                        rhs=xc[i][:, g * P : (g + 1) * P].bitcast(FP8X4),
                        rhs_scale=xs[i][:, g * P : (g + 1) * P],
                        start=(g == 0),
                        stop=(g == PASSES - 1),
                    )

        def leave(m, i, h):
            if h == 0:
                yg[m, i] = work.tile([P, 1024], BF16, name="yg", align_bytes=64)
            dst = yg[m, i][:, h * 512 : (h + 1) * 512].rearrange("p (n t) -> p n t", t=4)
            bank = yp[m, i, h][:].rearrange("p (t n) -> p n t", t=4)
            if (m + str(i), h) in EXIT_V:
                nc.vector.tensor_copy(out=dst, in_=bank)
            else:
                nc.scalar.copy(dst, bank)

        def quant_y(m, i):
            b, j = divmod(i, PER_BATCH)
            if m == "Q":
                nc.vector.quantize_mx(out=qc[i][:].bitcast(FP8X4), scales=qs[i][:], in_=yg[m, i][:])
            else:
                for h in range(2):
                    cols = slice(h * S + j * P, h * S + (j + 1) * P)
                    nc.vector.quantize_mx(out=kc[b][:, cols].bitcast(FP8X4), scales=ks[b][:, cols], in_=yg[m, i][:, h * 512 : (h + 1) * 512])

        def score(i):
            b = i // PER_BATCH
            sp[i] = banks.tile([P, S], F32, name="bank")
            for h in range(2):
                nc.tensor.matmul_mx(
                    out=sp[i][:],
                    lhsT=qc[i][:, h * P : (h + 1) * P].bitcast(FP8X4),
                    lhsT_scale=qs[i][:, h * P : (h + 1) * P],
                    rhs=kc[b][:, h * S : (h + 1) * S].bitcast(FP8X4),
                    rhs_scale=ks[b][:, h * S : (h + 1) * S],
                    start=(h == 0),
                    stop=(h == 1),
                )

        def row_max(i):
            mx = soft.tile([P, 1], F32, name="mx")
            nb = soft.tile([P, 1], F32, name="nb")
            nc.vector.tensor_reduce(out=mx[:], in_=sp[i][:], axis=AX.X, op=ALU.max)
            ex[i] = [mx, nb]

        def exps(i):
            mx, nb = ex[i]
            nc.scalar.mul(nb[:], mx[:], -INV)
            e = soft.tile([P, S], F32, name="e")
            sm = soft.tile([P, 1], F32, name="sm")
            nc.scalar.activation(out=e[:], in_=sp[i][:], func=ACT.Exp, bias=nb[:], scale=INV, accum_out=sm[:])
            ex[i] = [e, sm]

        def invert(i):
            e, sm = ex[i]
            rc = soft.tile([P, 1], F32, name="rc")
            nc.vector.reciprocal(rc[:], sm[:])
            ex[i] = (e, rc)

        def finish(i):
            e, rc = ex[i]
            o = soft.tile([P, S], F32, name="o")
            if i in NORM_SPLIT:
                lo, hi = slice(0, NORM_COLS), slice(NORM_COLS, S)
                nc.scalar.activation(out=o[:, hi], in_=e[:, hi], func=ACT.Copy, scale=rc[:])
                nc.vector.tensor_scalar(out=o[:, lo], in0=e[:, lo], scalar1=rc[:], scalar2=None, op0=ALU.mult)
                nc.scalar.dma_start(out=out_rows[i * P : (i + 1) * P, hi], in_=o[:, hi])
                nc.sync.dma_start(out=out_rows[i * P : (i + 1) * P, lo], in_=o[:, lo])
                return
            if i in NORM_G:
                nc.gpsimd.tensor_scalar(out=o[:], in0=e[:], scalar1=rc[:], scalar2=0.0, op0=ALU.mult, op1=ALU.add)
            else:
                nc.vector.tensor_scalar(out=o[:], in0=e[:], scalar1=rc[:], scalar2=None, op0=ALU.mult)
            nc.sync.dma_start(out=out_rows[i * P : (i + 1) * P, :], in_=o[:])

        ctx.enter_context(tc.manual_schedule())
        make_identity(nc, ident[:])
        nc.vector.memset(warm[:], 0.0)
        nc.scalar.activation(out=warm_out[:], in_=warm[:], func=ACT.Exp)
        nc.vector.memset(raw_s["K"][:].bitcast(I32), 0)
        nc.vector.memset(zeros[:], 0.0)
        nc.vector.memset(raw_s["Q"][:].bitcast(I32), 0)
        load_x(0)
        nc.scalar.dma_start(out=scale_t[:].rearrange("p (g t) -> p g t", t=4), in_=x_scale.rearrange("a b (g p t) -> p (a b g) t", p=P, t=4))
        for i in range(1, XFIRST):
            load_x(i)
        load_s("K")
        load_w("K", 0)
        load_w("K", 1)
        load_x(XFIRST)
        load_w("Q", 0)
        load_w("Q", 1)
        load_s("Q")
        for i in range(XFIRST + 1, TILES):
            load_x(i)
        for m in "KQ":
            for h in range(2):
                permute_s(m, h)

        pending = {}

        def later(n, fn, *args):
            pending.setdefault(n, []).append((fn, args))

        for n, op in enumerate(SEQ):
            kind, i = op[0], int(op[1:] or 0)
            if kind == "D":
                continue
            if kind == "T":
                later(max(n - LAG_CAST, -1), cast, i)
                later(n + LAG_SCALE, scale, i, 0)
                later(n + LAG_SCALE, scale, i, 1)
                if i == 0:
                    later(n + LAG_SCALE, permute, "K", 0)
                later(n + LAG_SCALE, quant_x, i)
                if i == 0:
                    later(n + LAG_SCALE, permute, "K", 1)
            elif kind == "S":
                later(n + LAG_MAX, row_max, i)
                later(n + LAG_MAX + LAG_EXP, exps, i)
                later(n + LAG_MAX + LAG_EXP + LAG_INV, invert, i)
                later(n + LAG_MAX + LAG_EXP + LAG_INV + LAG_NORM, finish, i)
            else:
                later(n + LAG_QUANT, quant_y, kind, i)

        def run_pending(n):
            for fn, args in pending.get(n, []):
                fn(*args)

        later(PERM_Q, permute, "Q", 0)
        later(PERM_Q, permute, "Q", 1)
        run_pending(-1)
        for n, op in enumerate(SEQ):
            kind, i = op[0], int(op[1:] or 0)
            if kind == "D":
                nc.tensor.matmul(dummy[:], zeros[:, 0:P], zeros[:], start=True, stop=True)
            elif kind == "T":
                turn(i)
            elif kind == "S":
                score(i)
            else:
                for h in range(2):
                    project(kind, i, h)
                    leave(kind, i, h)
            run_pending(n)
        for n in range(len(SEQ), len(SEQ) + 9):
            run_pending(n)
